import numpy as np
import ml_dtypes

BF16 = ml_dtypes.bfloat16


def bf(x):
    return np.asarray(x, np.float32).astype(BF16)


def f32(x):
    return np.asarray(x, np.float32)


def f64(x):
    return np.asarray(x).astype(np.float64)


def striped(idx):
    return np.tile(idx.reshape(-1, 16).T, (8, 1))


K, S, N, F = 512, 4096, 2048, 128
RT = 2
BN_EPS = 1e-5
NORM_EPS = 1e-12


def softmax_k(s):
    e = np.exp(s - s.max(axis=0, keepdims=True))
    return e / e.sum(axis=0, keepdims=True)


def squash(a):
    q = np.sum(a * a, axis=1, keepdims=True)
    return q / (1.0 + q) * (a / np.sqrt(q))


def setup_inputs():
    lim = np.sqrt(2.0) * np.sqrt(6.0 / (F + K))
    return {"base": f32(np.random.standard_normal((K, S))), "x": bf(np.random.standard_normal((N, F))), "adj_t": bf(np.random.uniform(0.0, 1.0, (N, N)) * np.sqrt(3.0 / N)), "w": bf(np.random.uniform(-lim, lim, (F, K))), "b": f32(0.1 * np.random.standard_normal((K, 1))), "offs": striped(np.random.permutation(S)[:N])}


def reference(base, x, adj_t, w, b, offs):
    idx = offs[:16].T.reshape(-1)
    xs = f64(x)
    h = xs.T @ f64(adj_t)
    u = f64(w).T @ h + f64(b)
    nrm = np.sqrt(np.sum(u * u, axis=0, keepdims=True))
    v = np.maximum(u / np.maximum(nrm, NORM_EPS), 0.0)
    mean = v.mean(axis=0, keepdims=True)
    var = np.mean((v - mean) ** 2, axis=0, keepdims=True)
    s = (v - mean) / np.sqrt(var + BN_EPS)
    for t in range(RT):
        p = softmax_k(s)
        cap = squash(p @ xs)
        s = s + cap @ xs.T
    res = f64(base).copy()
    res[:, idx] = s
    return res

@@ -1,0 +1,222 @@
+from contextlib import ExitStack
+
+import concourse.mybir as mybir
+from concourse.masks import make_identity
+
+F32 = mybir.dt.float32
+BF16 = mybir.dt.bfloat16
+U16 = mybir.dt.uint16
+ALU = mybir.AluOpType
+FN = mybir.ActivationFunctionType
+
+P = 128
+K, S, N, F = 512, 4096, 2048, 128
+NB = N // P
+KB = K // P
+CH = 512
+NCH = N // CH
+BPC = CH // P
+BN_EPS = 1e-5
+NORM_EPS = 1e-12
+
+FLOPS = 2 * F * N * N + 2 * F * K * N + 2 * (2 * K * N * F + 2 * K * N * F)
+
+
+def tile_routingassignment_b_kernel(tc, base, x, adj_t, w, b, offs, out):
+    nc = tc.nc
+    with ExitStack() as ctx:
+        held = ctx.enter_context(tc.tile_pool(name="held", bufs=1))
+        two = ctx.enter_context(tc.tile_pool(name="two", bufs=2))
+        three = ctx.enter_context(tc.tile_pool(name="three", bufs=3))
+        psum_a = ctx.enter_context(tc.psum_pool(name="psum_a", bufs=1))
+        psum_h = ctx.enter_context(tc.psum_pool(name="psum_h", bufs=2))
+        psum_w = ctx.enter_context(tc.psum_pool(name="psum_w", bufs=5))
+
+        x_sb = held.tile([P, NB, F], BF16, name="x_sb")
+        nc.scalar.dma_start(x_sb[:], x.rearrange("(nb p) f -> p nb f", p=P))
+        w_sb = held.tile([F, K], BF16, name="w_sb")
+        nc.scalar.dma_start(w_sb[:], w)
+        b_row = held.tile([1, K], F32, name="b_row")
+        nc.scalar.dma_start(b_row[:], b.rearrange("k one -> one k"))
+        offsets = held.tile([P, N // 16], U16, name="offsets")
+
+        ident_f = held.tile([P, P], F32, name="ident_f")
+        make_identity(nc, ident_f[:])
+        ident_b = held.tile([P, P], BF16, name="ident_b")
+        make_identity(nc, ident_b[:])
+        minus_half = held.tile([P, BPC], F32, name="minus_half")
+        nc.vector.memset(minus_half[:], -0.5)
+        plus_half = held.tile([P, KB], F32, name="plus_half")
+        nc.vector.memset(plus_half[:], 0.5)
+
+        ones_row = held.tile([1, P], F32, name="ones_row")
+        nc.vector.memset(ones_row[:], 1.0)
+        b_ps = psum_w.tile([P, K], F32, name="b_ps", tag="w")
+        nc.tensor.matmul(b_ps[:], lhsT=ones_row[:], rhs=b_row[:], start=True, stop=True)
+        b_all = held.tile([P, K], F32, name="b_all")
+        nc.vector.tensor_copy(b_all[:], b_ps[:])
+
+        ssq = held.tile([P, NB], F32, name="ssq")
+        stats = held.tile([P, NB, 6], F32, name="stats")
+        mean_var = held.tile([P, NB, 2], F32, name="mean_var")
+        gain = held.tile([P, NB], F32, name="gain")
+        shift = held.tile([P, NB], F32, name="shift")
+        top = held.tile([P, NB], F32, name="top")
+        minus_top = held.tile([P, NB], F32, name="minus_top")
+
+        x_t = held.tile([F, N], BF16, name="x_t")
+        logits = [held.tile([P, K], F32, name=f"logits{nb}") for nb in range(NB)]
+
+        def aggregate(adj_c):
+            h_ps = psum_h.tile([F, CH], F32, name="h_ps", tag="h")
+            for t in range(NB):
+                nc.tensor.matmul(h_ps[:], lhsT=x_sb[:, t, :], rhs=adj_c[:, t, :], start=(t == 0), stop=(t == NB - 1))
+            h_bf = two.tile([F, CH], BF16, name="h_bf")
+            nc.scalar.copy(h_bf[:], h_ps[:])
+            return h_bf
+
+        def linear_and_statistics(nb, h_bf):
+            r = nb % BPC
+            u_ps = psum_w.tile([P, K], F32, name="u_ps", tag="w")
+            nc.tensor.matmul(u_ps[:], lhsT=h_bf[:, r * P : (r + 1) * P], rhs=w_sb[:], start=True, stop=True)
+            u = two.tile([P, K], F32, name="u")
+            nc.vector.tensor_tensor(u[:], u_ps[:], b_all[:], ALU.add)
+            squares = two.tile([P, K], BF16, name="squares")
+            nc.scalar.activation(squares[:], u[:], FN.Square, accum_out=ssq[:, nb : nb + 1])
+            nc.vector.tensor_scalar_max(logits[nb][:], u[:], 0.0)
+            nc.vector.bn_stats(stats[:, nb, :], logits[nb][:])
+            nc.vector.bn_aggr(mean_var[:, nb, :], stats[:, nb, :])
+
+        def normalisation(c):
+            blocks = slice(c * BPC, (c + 1) * BPC)
+            spread = two.tile([P, BPC], F32, name="spread")
+            nc.vector.tensor_scalar(spread[:], ssq[:, blocks], BN_EPS, BN_EPS * NORM_EPS * NORM_EPS, ALU.mult, ALU.max)
+            nc.vector.tensor_tensor(spread[:], spread[:], mean_var[:, blocks, 1], ALU.add)
+            nc.gpsimd.tensor_tensor(gain[:, blocks], spread[:], minus_half[:], ALU.pow)
+            nc.vector.scalar_tensor_tensor(
+                shift[:, blocks], mean_var[:, blocks, 0], -1.0, gain[:, blocks], ALU.mult, ALU.mult
+            )
+
+        def weigh_and_sum(nb, a_ps, exponent, scale, bias):
+            e = three.tile([P, K], F32, name="e")
+            total = three.tile([P, 1], F32, name="total")
+            nc.scalar.activation(e[:], exponent, FN.Exp, bias=bias, scale=scale, accum_out=total[:])
+            inverse = three.tile([P, 1], F32, name="inverse")
+            nc.vector.reciprocal(inverse[:], total[:])
+            p = three.tile([P, K], BF16, name="p")
+            if nb % 2 == 0:
+                nc.scalar.activation(p[:], e[:], FN.Copy, scale=inverse[:])
+            else:
+                nc.vector.tensor_scalar_mul(p[:], e[:], inverse[:])
+            for kb in range(KB):
+                nc.tensor.matmul(
+                    a_ps[:, kb * F : (kb + 1) * F],
+                    lhsT=p[:, kb * P : (kb + 1) * P],
+                    rhs=x_sb[:, nb, :],
+                    start=(nb == 0 and kb == 0),
+                    stop=(nb == NB - 1 and kb == KB - 1),
+                )
+
+        def squash_factor(a_ps):
+            q = two.tile([P, KB], F32, name="q")
+            a_squares = two.tile([P, F], BF16, name="a_squares")
+            for kb in range(KB):
+                nc.scalar.activation(
+                    a_squares[:], a_ps[:, kb * F : (kb + 1) * F], FN.Square, accum_out=q[:, kb : kb + 1]
+                )
+            root = two.tile([P, KB], F32, name="root")
+            nc.gpsimd.tensor_tensor(root[:], q[:], plus_half[:], ALU.pow)
+            factor = two.tile([P, KB], F32, name="factor")
+            nc.vector.tensor_scalar_add(factor[:], q[:], 1.0)
+            nc.vector.reciprocal(factor[:], factor[:])
+            nc.vector.tensor_tensor(factor[:], factor[:], root[:], ALU.mult)
+            return factor
+
+        def capsules(a_ps, factor, kb, cap_t):
+            cap = two.tile([P, F], BF16, name="cap")
+            nc.vector.tensor_scalar_mul(cap[:], a_ps[:, kb * F : (kb + 1) * F], factor[:, kb : kb + 1])
+            cap_ps = psum_h.tile([F, P], BF16, name="cap_ps", tag="h")
+            nc.tensor.transpose(cap_ps[:], cap[:], ident_b[:])
+            nc.vector.tensor_copy(cap_t, cap_ps[:])
+
+        a0_ps = psum_a.tile([P, K], F32, name="a0_ps", tag="a")
+        with tc.tile_pool(name="adj", bufs=NCH) as adj_pool:
+            adj_runs = adj_t.rearrange("(t p) j -> p t j", p=P)
+            adj_chunks = []
+            for c in range(NCH):
+                adj_c = adj_pool.tile([P, NB, CH], BF16, name="adj_c")
+                for q in range(0, NB, BPC):
+                    nc.sync.dma_start(adj_c[:, q : q + BPC, :], adj_runs[:, q : q + BPC, c * CH : (c + 1) * CH])
+                adj_chunks.append(adj_c)
+            nc.sync.dma_start(offsets[:], offs)
+
+            h_bf = aggregate(adj_chunks[0])
+            for c in range(NCH):
+                x_ps = psum_w.tile([F, CH], BF16, name="x_ps", tag="w")
+                for r in range(BPC):
+                    nc.tensor.transpose(x_ps[:, r * P : (r + 1) * P], x_sb[:, c * BPC + r, :], ident_b[:])
+                nc.vector.tensor_copy(x_t[:, c * CH : (c + 1) * CH], x_ps[:])
+            for nb in range(BPC):
+                linear_and_statistics(nb, h_bf)
+            for c in range(NCH):
+                if c + 1 < NCH:
+                    h_bf = aggregate(adj_chunks[c + 1])
+                normalisation(c)
+                for nb in range(c * BPC, (c + 1) * BPC):
+                    if c + 1 < NCH:
+                        linear_and_statistics(nb + BPC, h_bf)
+                    weigh_and_sum(nb, a0_ps, logits[nb][:], gain[:, nb : nb + 1], shift[:, nb : nb + 1])
+
+        late = ctx.enter_context(tc.tile_pool(name="late", bufs=1))
+        windows = [late.tile([P, S], F32, name=f"window{kb}") for kb in range(KB)]
+        for kb in range(KB):
+            nc.sync.dma_start(windows[kb][:], base[kb * P : (kb + 1) * P, :])
+        s1_t = [late.tile([P, N], F32, name=f"s1_t{kb}") for kb in range(KB)]
+
+        factor0 = squash_factor(a0_ps)
+        cap0_t = held.tile([F, K], BF16, name="cap0_t")
+        for kb in range(KB):
+            capsules(a0_ps, factor0, kb, cap0_t[:, kb * P : (kb + 1) * P])
+
+        def transpose_s1(kb, c):
+            turned = psum_w.tile([P, CH], F32, name="turned", tag="w")
+            for r in range(BPC):
+                nc.tensor.transpose(
+                    turned[:, r * P : (r + 1) * P], logits[c * BPC + r][:, kb * P : (kb + 1) * P], ident_f[:]
+                )
+            nc.scalar.copy(s1_t[kb][:, c * CH : (c + 1) * CH], turned[:])
+
+        a1_ps = psum_a.tile([P, K], F32, name="a1_ps", tag="a")
+        for c in range(NCH):
+            for nb in range(c * BPC, (c + 1) * BPC):
+                step_ps = psum_w.tile([P, K], F32, name="step_ps", tag="w")
+                nc.tensor.matmul(step_ps[:], lhsT=x_t[:, nb * P : (nb + 1) * P], rhs=cap0_t[:], start=True, stop=True)
+                partial = two.tile([P, K], F32, name="partial")
+                nc.vector.scalar_tensor_tensor(
+                    partial[:], logits[nb][:], gain[:, nb : nb + 1], step_ps[:], ALU.mult, ALU.add
+                )
+                nc.vector.tensor_scalar(
+                    logits[nb][:], partial[:], shift[:, nb : nb + 1], None, ALU.add, ALU.max,
+                    accum_out=top[:, nb : nb + 1],
+                )
+                nc.scalar.mul(minus_top[:, nb : nb + 1], top[:, nb : nb + 1], -1.0)
+                weigh_and_sum(nb, a1_ps, logits[nb][:], 1.0, minus_top[:, nb : nb + 1])
+            transpose_s1(0, c)
+        factor1 = squash_factor(a1_ps)
+
+        for kb in range(KB):
+            cap1_t = two.tile([F, P], BF16, name="cap1_t")
+            capsules(a1_ps, factor1, kb, cap1_t[:])
+            if kb > 0:
+                for c in range(NCH):
+                    transpose_s1(kb, c)
+            last_step = late.tile([P, N], F32, name="last_step", bufs=2)
+            for c in range(NCH):
+                last_ps = psum_w.tile([P, CH], F32, name="last_ps", tag="w")
+                nc.tensor.matmul(
+                    last_ps[:], lhsT=cap1_t[:], rhs=x_t[:, c * CH : (c + 1) * CH],
+                    start=True, stop=True,
+                )
+                nc.scalar.copy(last_step[:, c * CH : (c + 1) * CH], last_ps[:])
+            nc.vector.tensor_tensor(windows[kb][:].indirect(offsets[:]), s1_t[kb][:], last_step[:], ALU.add)
+            nc.sync.dma_start(out[kb * P : (kb + 1) * P, :], windows[kb][:])

@@ -16,6 +16,10 @@ KB = K // P
 CH = 512
 NCH = N // CH
 BPC = CH // P
+HALF = CH // 2
+NH = N // HALF
+BPH = HALF // P
+AHEAD = 2
 BN_EPS = 1e-5
 NORM_EPS = 1e-12
 
@@ -29,8 +33,8 @@ def tile_routingassignment_b_kernel(tc, base, x, adj_t, w, b, offs, out):
         two = ctx.enter_context(tc.tile_pool(name="two", bufs=2))
         three = ctx.enter_context(tc.tile_pool(name="three", bufs=3))
         psum_a = ctx.enter_context(tc.psum_pool(name="psum_a", bufs=1))
-        psum_h = ctx.enter_context(tc.psum_pool(name="psum_h", bufs=2))
-        psum_w = ctx.enter_context(tc.psum_pool(name="psum_w", bufs=5))
+        psum_h = ctx.enter_context(tc.psum_pool(name="psum_h", bufs=AHEAD + 1))
+        psum_w = ctx.enter_context(tc.psum_pool(name="psum_w", bufs=4))
 
         x_sb = held.tile([P, NB, F], BF16, name="x_sb")
         nc.scalar.dma_start(x_sb[:], x.rearrange("(nb p) f -> p nb f", p=P))
@@ -44,7 +48,7 @@ def tile_routingassignment_b_kernel(tc, base, x, adj_t, w, b, offs, out):
         make_identity(nc, ident_f[:])
         ident_b = held.tile([P, P], BF16, name="ident_b")
         make_identity(nc, ident_b[:])
-        minus_half = held.tile([P, BPC], F32, name="minus_half")
+        minus_half = held.tile([P, BPH], F32, name="minus_half")
         nc.vector.memset(minus_half[:], -0.5)
         plus_half = held.tile([P, KB], F32, name="plus_half")
         nc.vector.memset(plus_half[:], 0.5)
@@ -67,16 +71,18 @@ def tile_routingassignment_b_kernel(tc, base, x, adj_t, w, b, offs, out):
         x_t = held.tile([F, N], BF16, name="x_t")
         logits = [held.tile([P, K], F32, name=f"logits{nb}") for nb in range(NB)]
 
-        def aggregate(adj_c):
-            h_ps = psum_h.tile([F, CH], F32, name="h_ps", tag="h")
+        def aggregate(adj_half):
+            h_ps = psum_h.tile([F, HALF], F32, name="h_ps", tag="h")
             for t in range(NB):
-                nc.tensor.matmul(h_ps[:], lhsT=x_sb[:, t, :], rhs=adj_c[:, t, :], start=(t == 0), stop=(t == NB - 1))
-            h_bf = two.tile([F, CH], BF16, name="h_bf")
+                nc.tensor.matmul(
+                    h_ps[:], lhsT=x_sb[:, t, :], rhs=adj_half[:, t, :], start=(t == 0), stop=(t == NB - 1)
+                )
+            h_bf = three.tile([F, HALF], BF16, name="h_bf")
             nc.scalar.copy(h_bf[:], h_ps[:])
             return h_bf
 
         def linear_and_statistics(nb, h_bf):
-            r = nb % BPC
+            r = nb % BPH
             u_ps = psum_w.tile([P, K], F32, name="u_ps", tag="w")
             nc.tensor.matmul(u_ps[:], lhsT=h_bf[:, r * P : (r + 1) * P], rhs=w_sb[:], start=True, stop=True)
             u = two.tile([P, K], F32, name="u")
@@ -87,9 +93,9 @@ def tile_routingassignment_b_kernel(tc, base, x, adj_t, w, b, offs, out):
             nc.vector.bn_stats(stats[:, nb, :], logits[nb][:])
             nc.vector.bn_aggr(mean_var[:, nb, :], stats[:, nb, :])
 
-        def normalisation(c):
-            blocks = slice(c * BPC, (c + 1) * BPC)
-            spread = two.tile([P, BPC], F32, name="spread")
+        def normalisation(hc):
+            blocks = slice(hc * BPH, (hc + 1) * BPH)
+            spread = two.tile([P, BPH], F32, name="spread")
             nc.vector.tensor_scalar(spread[:], ssq[:, blocks], BN_EPS, BN_EPS * NORM_EPS * NORM_EPS, ALU.mult, ALU.max)
             nc.vector.tensor_tensor(spread[:], spread[:], mean_var[:, blocks, 1], ALU.add)
             nc.gpsimd.tensor_tensor(gain[:, blocks], spread[:], minus_half[:], ALU.pow)
@@ -145,26 +151,30 @@ def tile_routingassignment_b_kernel(tc, base, x, adj_t, w, b, offs, out):
             adj_chunks = []
             for c in range(NCH):
                 adj_c = adj_pool.tile([P, NB, CH], BF16, name="adj_c")
-                for q in range(0, NB, BPC):
-                    nc.sync.dma_start(adj_c[:, q : q + BPC, :], adj_runs[:, q : q + BPC, c * CH : (c + 1) * CH])
+                parts = [(0, HALF), (HALF, CH)] if c == 0 else [(0, CH)]
+                rows = BPC * len(parts)
+                for lo, hi in parts:
+                    for q in range(0, NB, rows):
+                        nc.sync.dma_start(adj_c[:, q : q + rows, lo:hi], adj_runs[:, q : q + rows, c * CH + lo : c * CH + hi])
                 adj_chunks.append(adj_c)
             nc.sync.dma_start(offsets[:], offs)
 
-            h_bf = aggregate(adj_chunks[0])
+            halves = [adj_chunks[hc // 2][:, :, (hc % 2) * HALF : (hc % 2 + 1) * HALF] for hc in range(NH)]
+            h_bfs = [aggregate(halves[hc]) for hc in range(AHEAD)]
             for c in range(NCH):
                 x_ps = psum_w.tile([F, CH], BF16, name="x_ps", tag="w")
                 for r in range(BPC):
                     nc.tensor.transpose(x_ps[:, r * P : (r + 1) * P], x_sb[:, c * BPC + r, :], ident_b[:])
                 nc.vector.tensor_copy(x_t[:, c * CH : (c + 1) * CH], x_ps[:])
-            for nb in range(BPC):
-                linear_and_statistics(nb, h_bf)
-            for c in range(NCH):
-                if c + 1 < NCH:
-                    h_bf = aggregate(adj_chunks[c + 1])
-                normalisation(c)
-                for nb in range(c * BPC, (c + 1) * BPC):
-                    if c + 1 < NCH:
-                        linear_and_statistics(nb + BPC, h_bf)
+            for nb in range(BPH):
+                linear_and_statistics(nb, h_bfs[0])
+            for hc in range(NH):
+                if hc + AHEAD < NH:
+                    h_bfs.append(aggregate(halves[hc + AHEAD]))
+                normalisation(hc)
+                for nb in range(hc * BPH, (hc + 1) * BPH):
+                    if hc + 1 < NH:
+                        linear_and_statistics(nb + BPH, h_bfs[hc + 1])
                     weigh_and_sum(nb, a0_ps, logits[nb][:], gain[:, nb : nb + 1], shift[:, nb : nb + 1])
 
         late = ctx.enter_context(tc.tile_pool(name="late", bufs=1))

@@ -1,3 +1,4 @@
+import math
 from contextlib import ExitStack
 
 import concourse.mybir as mybir
@@ -19,7 +20,6 @@ BPC = CH // P
 HALF = CH // 2
 NH = N // HALF
 BPH = HALF // P
-AHEAD = 2
 BN_EPS = 1e-5
 NORM_EPS = 1e-12
 
@@ -31,9 +31,9 @@ def tile_routingassignment_b_kernel(tc, base, x, adj_t, w, b, offs, out):
     with ExitStack() as ctx:
         held = ctx.enter_context(tc.tile_pool(name="held", bufs=1))
         two = ctx.enter_context(tc.tile_pool(name="two", bufs=2))
-        three = ctx.enter_context(tc.tile_pool(name="three", bufs=3))
+        four = ctx.enter_context(tc.tile_pool(name="four", bufs=4))
         psum_a = ctx.enter_context(tc.psum_pool(name="psum_a", bufs=1))
-        psum_h = ctx.enter_context(tc.psum_pool(name="psum_h", bufs=AHEAD + 1))
+        psum_h = ctx.enter_context(tc.psum_pool(name="psum_h", bufs=3))
         psum_w = ctx.enter_context(tc.psum_pool(name="psum_w", bufs=4))
 
         x_sb = held.tile([P, NB, F], BF16, name="x_sb")
@@ -63,65 +63,37 @@ def tile_routingassignment_b_kernel(tc, base, x, adj_t, w, b, offs, out):
         ssq = held.tile([P, NB], F32, name="ssq")
         stats = held.tile([P, NB, 6], F32, name="stats")
         mean_var = held.tile([P, NB, 2], F32, name="mean_var")
+        spread = held.tile([P, NB], F32, name="spread")
         gain = held.tile([P, NB], F32, name="gain")
         shift = held.tile([P, NB], F32, name="shift")
         top = held.tile([P, NB], F32, name="top")
         minus_top = held.tile([P, NB], F32, name="minus_top")
+        total = held.tile([P, NB], F32, name="total")
+        inverse = held.tile([P, NB], F32, name="inverse")
 
         x_t = held.tile([F, N], BF16, name="x_t")
         logits = [held.tile([P, K], F32, name=f"logits{nb}") for nb in range(NB)]
 
-        def aggregate(adj_half):
-            h_ps = psum_h.tile([F, HALF], F32, name="h_ps", tag="h")
-            for t in range(NB):
-                nc.tensor.matmul(
-                    h_ps[:], lhsT=x_sb[:, t, :], rhs=adj_half[:, t, :], start=(t == 0), stop=(t == NB - 1)
-                )
-            h_bf = three.tile([F, HALF], BF16, name="h_bf")
-            nc.scalar.copy(h_bf[:], h_ps[:])
-            return h_bf
+        pairs = [(2 * h, 2 * h + 1) for h in range(NH)]
 
-        def linear_and_statistics(nb, h_bf):
-            r = nb % BPH
-            u_ps = psum_w.tile([P, K], F32, name="u_ps", tag="w")
-            nc.tensor.matmul(u_ps[:], lhsT=h_bf[:, r * P : (r + 1) * P], rhs=w_sb[:], start=True, stop=True)
-            u = two.tile([P, K], F32, name="u")
-            nc.vector.tensor_tensor(u[:], u_ps[:], b_all[:], ALU.add)
-            squares = two.tile([P, K], BF16, name="squares")
-            nc.scalar.activation(squares[:], u[:], FN.Square, accum_out=ssq[:, nb : nb + 1])
-            nc.vector.tensor_scalar_max(logits[nb][:], u[:], 0.0)
-            nc.vector.bn_stats(stats[:, nb, :], logits[nb][:])
-            nc.vector.bn_aggr(mean_var[:, nb, :], stats[:, nb, :])
+        def columns(pair):
+            return slice(pair[0], pair[1] + 1)
 
-        def normalisation(hc):
-            blocks = slice(hc * BPH, (hc + 1) * BPH)
-            spread = two.tile([P, BPH], F32, name="spread")
-            nc.vector.tensor_scalar(spread[:], ssq[:, blocks], BN_EPS, BN_EPS * NORM_EPS * NORM_EPS, ALU.mult, ALU.max)
-            nc.vector.tensor_tensor(spread[:], spread[:], mean_var[:, blocks, 1], ALU.add)
-            nc.gpsimd.tensor_tensor(gain[:, blocks], spread[:], minus_half[:], ALU.pow)
-            nc.vector.scalar_tensor_tensor(
-                shift[:, blocks], mean_var[:, blocks, 0], -1.0, gain[:, blocks], ALU.mult, ALU.mult
-            )
-
-        def weigh_and_sum(nb, a_ps, exponent, scale, bias):
-            e = three.tile([P, K], F32, name="e")
-            total = three.tile([P, 1], F32, name="total")
-            nc.scalar.activation(e[:], exponent, FN.Exp, bias=bias, scale=scale, accum_out=total[:])
-            inverse = three.tile([P, 1], F32, name="inverse")
-            nc.vector.reciprocal(inverse[:], total[:])
-            p = three.tile([P, K], BF16, name="p")
-            if nb % 2 == 0:
-                nc.scalar.activation(p[:], e[:], FN.Copy, scale=inverse[:])
-            else:
-                nc.vector.tensor_scalar_mul(p[:], e[:], inverse[:])
-            for kb in range(KB):
-                nc.tensor.matmul(
-                    a_ps[:, kb * F : (kb + 1) * F],
-                    lhsT=p[:, kb * P : (kb + 1) * P],
-                    rhs=x_sb[:, nb, :],
-                    start=(nb == 0 and kb == 0),
-                    stop=(nb == NB - 1 and kb == KB - 1),
-                )
+        def divide_and_sum(blocks, exps, a_ps):
+            for nb in blocks:
+                p = four.tile([P, K], BF16, name="p")
+                if nb % 2 == 0:
+                    nc.scalar.activation(p[:], exps[nb][:], FN.Copy, scale=inverse[:, nb : nb + 1])
+                else:
+                    nc.vector.tensor_scalar_mul(p[:], exps[nb][:], inverse[:, nb : nb + 1])
+                for kb in range(KB):
+                    nc.tensor.matmul(
+                        a_ps[:, kb * F : (kb + 1) * F],
+                        lhsT=p[:, kb * P : (kb + 1) * P],
+                        rhs=x_sb[:, nb, :],
+                        start=(nb == 0 and kb == 0),
+                        stop=(nb == NB - 1 and kb == KB - 1),
+                    )
 
         def squash_factor(a_ps):
             q = two.tile([P, KB], F32, name="q")
@@ -159,23 +131,104 @@ def tile_routingassignment_b_kernel(tc, base, x, adj_t, w, b, offs, out):
                 adj_chunks.append(adj_c)
             nc.sync.dma_start(offsets[:], offs)
 
-            halves = [adj_chunks[hc // 2][:, :, (hc % 2) * HALF : (hc % 2 + 1) * HALF] for hc in range(NH)]
-            h_bfs = [aggregate(halves[hc]) for hc in range(AHEAD)]
-            for c in range(NCH):
-                x_ps = psum_w.tile([F, CH], BF16, name="x_ps", tag="w")
-                for r in range(BPC):
-                    nc.tensor.transpose(x_ps[:, r * P : (r + 1) * P], x_sb[:, c * BPC + r, :], ident_b[:])
-                nc.vector.tensor_copy(x_t[:, c * CH : (c + 1) * CH], x_ps[:])
-            for nb in range(BPH):
-                linear_and_statistics(nb, h_bfs[0])
-            for hc in range(NH):
-                if hc + AHEAD < NH:
-                    h_bfs.append(aggregate(halves[hc + AHEAD]))
-                normalisation(hc)
-                for nb in range(hc * BPH, (hc + 1) * BPH):
-                    if hc + 1 < NH:
-                        linear_and_statistics(nb + BPH, h_bfs[hc + 1])
-                    weigh_and_sum(nb, a0_ps, logits[nb][:], gain[:, nb : nb + 1], shift[:, nb : nb + 1])
+            h_pss, h_bfs, u_pss, us, exps = {}, {}, {}, {}, {}
+
+            def aggregate(hc):
+                adj_half = adj_chunks[hc // 2][:, :, (hc % 2) * HALF : (hc % 2 + 1) * HALF]
+                h_pss[hc] = psum_h.tile([F, HALF], F32, name="h_ps", tag="h")
+                for t in range(NB):
+                    nc.tensor.matmul(
+                        h_pss[hc][:], lhsT=x_sb[:, t, :], rhs=adj_half[:, t, :], start=(t == 0), stop=(t == NB - 1)
+                    )
+
+            def round_h(hc):
+                h_bfs[hc] = four.tile([F, HALF], BF16, name="h_bf")
+                nc.scalar.copy(h_bfs[hc][:], h_pss[hc][:])
+
+            def linear(hc):
+                for r, nb in enumerate(pairs[hc]):
+                    u_pss[nb] = psum_w.tile([P, K], F32, name="u_ps", tag="w")
+                    nc.tensor.matmul(
+                        u_pss[nb][:], lhsT=h_bfs[hc][:, r * P : (r + 1) * P], rhs=w_sb[:], start=True, stop=True
+                    )
+
+            def add_bias(hc):
+                for nb in pairs[hc]:
+                    us[nb] = four.tile([P, K], F32, name="u")
+                    nc.vector.tensor_tensor(us[nb][:], u_pss[nb][:], b_all[:], ALU.add)
+
+            def sums_of_squares(hc):
+                for nb in pairs[hc]:
+                    squares = four.tile([P, K], BF16, name="squares")
+                    nc.scalar.activation(
+                        squares[:], us[nb][:], FN.Square, scale=math.sqrt(BN_EPS), accum_out=ssq[:, nb : nb + 1]
+                    )
+
+            def relu(hc):
+                for nb in pairs[hc]:
+                    nc.vector.tensor_scalar_max(logits[nb][:], us[nb][:], 0.0)
+
+            def statistics(hc):
+                for nb in pairs[hc]:
+                    nc.vector.bn_stats(stats[:, nb, :], logits[nb][:])
+
+            def mean_and_variance(hc):
+                for nb in pairs[hc]:
+                    nc.vector.bn_aggr(mean_var[:, nb, :], stats[:, nb, :])
+
+            def gains(hc):
+                blocks = columns(pairs[hc])
+                nc.vector.scalar_tensor_tensor(
+                    spread[:, blocks], ssq[:, blocks], BN_EPS * NORM_EPS * NORM_EPS, mean_var[:, blocks, 1],
+                    ALU.max, ALU.add,
+                )
+                nc.gpsimd.tensor_tensor(gain[:, blocks], spread[:, blocks], minus_half[:], ALU.pow)
+
+            def shifts(hc):
+                blocks = columns(pairs[hc])
+                nc.vector.scalar_tensor_tensor(
+                    shift[:, blocks], mean_var[:, blocks, 0], -1.0, gain[:, blocks], ALU.mult, ALU.mult
+                )
+
+            def exponentials(hc):
+                for nb in pairs[hc]:
+                    exps[nb] = four.tile([P, K], F32, name="e")
+                    nc.scalar.activation(
+                        exps[nb][:], logits[nb][:], FN.Exp, bias=shift[:, nb : nb + 1], scale=gain[:, nb : nb + 1],
+                        accum_out=total[:, nb : nb + 1],
+                    )
+
+            def inverse_sums(hc):
+                nc.vector.reciprocal(inverse[:, columns(pairs[hc])], total[:, columns(pairs[hc])])
+
+            def divide(hc):
+                divide_and_sum(pairs[hc], exps, a0_ps)
+
+            stages = [
+                (linear, 1),
+                (aggregate, 2),
+                (add_bias, 0),
+                (gains, -1),
+                (sums_of_squares, 0),
+                (inverse_sums, -2),
+                (relu, 0),
+                (divide, -2),
+                (statistics, 0),
+                (shifts, -1),
+                (exponentials, -1),
+                (round_h, 2),
+                (mean_and_variance, 0),
+            ]
+            for turn in range(-2, NH + 2):
+                for stage, ahead in stages:
+                    if 0 <= turn + ahead < NH:
+                        stage(turn + ahead)
+
+        for c in range(NCH):
+            x_ps = psum_w.tile([F, CH], BF16, name="x_ps", tag="w")
+            for r in range(BPC):
+                nc.tensor.transpose(x_ps[:, r * P : (r + 1) * P], x_sb[:, c * BPC + r, :], ident_b[:])
+            nc.vector.tensor_copy(x_t[:, c * CH : (c + 1) * CH], x_ps[:])
 
         late = ctx.enter_context(tc.tile_pool(name="late", bufs=1))
         windows = [late.tile([P, S], F32, name=f"window{kb}") for kb in range(KB)]
@@ -189,7 +242,7 @@ def tile_routingassignment_b_kernel(tc, base, x, adj_t, w, b, offs, out):
             capsules(a0_ps, factor0, kb, cap0_t[:, kb * P : (kb + 1) * P])
 
         def transpose_s1(kb, c):
-            turned = psum_w.tile([P, CH], F32, name="turned", tag="w")
+            turned = psum_h.tile([P, CH], F32, name="turned", tag="h")
             for r in range(BPC):
                 nc.tensor.transpose(
                     turned[:, r * P : (r + 1) * P], logits[c * BPC + r][:, kb * P : (kb + 1) * P], ident_f[:]
@@ -201,7 +254,7 @@ def tile_routingassignment_b_kernel(tc, base, x, adj_t, w, b, offs, out):
             for nb in range(c * BPC, (c + 1) * BPC):
                 step_ps = psum_w.tile([P, K], F32, name="step_ps", tag="w")
                 nc.tensor.matmul(step_ps[:], lhsT=x_t[:, nb * P : (nb + 1) * P], rhs=cap0_t[:], start=True, stop=True)
-                partial = two.tile([P, K], F32, name="partial")
+                partial = four.tile([P, K], F32, name="partial")
                 nc.vector.scalar_tensor_tensor(
                     partial[:], logits[nb][:], gain[:, nb : nb + 1], step_ps[:], ALU.mult, ALU.add
                 )
@@ -210,7 +263,13 @@ def tile_routingassignment_b_kernel(tc, base, x, adj_t, w, b, offs, out):
                     accum_out=top[:, nb : nb + 1],
                 )
                 nc.scalar.mul(minus_top[:, nb : nb + 1], top[:, nb : nb + 1], -1.0)
-                weigh_and_sum(nb, a1_ps, logits[nb][:], 1.0, minus_top[:, nb : nb + 1])
+                exps[nb] = four.tile([P, K], F32, name="e")
+                nc.scalar.activation(
+                    exps[nb][:], logits[nb][:], FN.Exp, bias=minus_top[:, nb : nb + 1], scale=1.0,
+                    accum_out=total[:, nb : nb + 1],
+                )
+                nc.vector.reciprocal(inverse[:, nb : nb + 1], total[:, nb : nb + 1])
+                divide_and_sum((nb,), exps, a1_ps)
             transpose_s1(0, c)
         factor1 = squash_factor(a1_ps)
 

@@ -82,10 +82,7 @@ def tile_routingassignment_b_kernel(tc, base, x, adj_t, w, b, offs, out):
         def divide_and_sum(blocks, exps, a_ps):
             for nb in blocks:
                 p = four.tile([P, K], BF16, name="p")
-                if nb % 2 == 0:
-                    nc.scalar.activation(p[:], exps[nb][:], FN.Copy, scale=inverse[:, nb : nb + 1])
-                else:
-                    nc.vector.tensor_scalar_mul(p[:], exps[nb][:], inverse[:, nb : nb + 1])
+                nc.gpsimd.tensor_scalar(p[:], exps[nb][:], inverse[:, nb : nb + 1], 0.0, ALU.mult, ALU.add)
                 for kb in range(KB):
                     nc.tensor.matmul(
                         a_ps[:, kb * F : (kb + 1) * F],

@@ -36,12 +36,14 @@ def tile_routingassignment_b_kernel(tc, base, x, adj_t, w, b, offs, out):
         psum_h = ctx.enter_context(tc.psum_pool(name="psum_h", bufs=3))
         psum_w = ctx.enter_context(tc.psum_pool(name="psum_w", bufs=4))
 
-        x_sb = held.tile([P, NB, F], BF16, name="x_sb")
-        nc.scalar.dma_start(x_sb[:], x.rearrange("(nb p) f -> p nb f", p=P))
-        w_sb = held.tile([F, K], BF16, name="w_sb")
-        nc.scalar.dma_start(w_sb[:], w)
         b_row = held.tile([1, K], F32, name="b_row")
         nc.scalar.dma_start(b_row[:], b.rearrange("k one -> one k"))
+        x_sb = held.tile([P, NB, F], BF16, name="x_sb")
+        x_blocks = x.rearrange("(nb p) f -> p nb f", p=P)
+        for lo in (0, NB // 2):
+            nc.scalar.dma_start(x_sb[:, lo : lo + NB // 2, :], x_blocks[:, lo : lo + NB // 2, :])
+        w_sb = held.tile([F, K], BF16, name="w_sb")
+        nc.scalar.dma_start(w_sb[:], w)
         offsets = held.tile([P, N // 16], U16, name="offsets")
 
         ident_f = held.tile([P, P], F32, name="ident_f")
@@ -79,10 +81,17 @@ def tile_routingassignment_b_kernel(tc, base, x, adj_t, w, b, offs, out):
         def columns(pair):
             return slice(pair[0], pair[1] + 1)
 
+        def run(stage, hc):
+            if 0 <= hc < NH:
+                stage(hc)
+
         def divide_and_sum(blocks, exps, a_ps):
             for nb in blocks:
                 p = four.tile([P, K], BF16, name="p")
-                nc.gpsimd.tensor_scalar(p[:], exps[nb][:], inverse[:, nb : nb + 1], 0.0, ALU.mult, ALU.add)
+                if nb in pairs[-1]:
+                    nc.vector.tensor_scalar_mul(p[:], exps[nb][:], inverse[:, nb : nb + 1])
+                else:
+                    nc.gpsimd.tensor_scalar(p[:], exps[nb][:], inverse[:, nb : nb + 1], 0.0, ALU.mult, ALU.add)
                 for kb in range(KB):
                     nc.tensor.matmul(
                         a_ps[:, kb * F : (kb + 1) * F],
@@ -92,27 +101,30 @@ def tile_routingassignment_b_kernel(tc, base, x, adj_t, w, b, offs, out):
                         stop=(nb == NB - 1 and kb == KB - 1),
                     )
 
-        def squash_factor(a_ps):
-            q = two.tile([P, KB], F32, name="q")
-            a_squares = two.tile([P, F], BF16, name="a_squares")
-            for kb in range(KB):
+        def squash_factor(a_ps, q, factor, first, last):
+            blocks = slice(first, last)
+            for kb in range(first, last):
+                a_squares = two.tile([P, F], BF16, name="a_squares")
                 nc.scalar.activation(
                     a_squares[:], a_ps[:, kb * F : (kb + 1) * F], FN.Square, accum_out=q[:, kb : kb + 1]
                 )
             root = two.tile([P, KB], F32, name="root")
-            nc.gpsimd.tensor_tensor(root[:], q[:], plus_half[:], ALU.pow)
-            factor = two.tile([P, KB], F32, name="factor")
-            nc.vector.tensor_scalar_add(factor[:], q[:], 1.0)
-            nc.vector.reciprocal(factor[:], factor[:])
-            nc.vector.tensor_tensor(factor[:], factor[:], root[:], ALU.mult)
-            return factor
+            nc.gpsimd.tensor_tensor(root[:, blocks], q[:, blocks], plus_half[:, blocks], ALU.pow)
+            nc.vector.tensor_scalar_add(factor[:, blocks], q[:, blocks], 1.0)
+            nc.vector.reciprocal(factor[:, blocks], factor[:, blocks])
+            nc.vector.tensor_tensor(factor[:, blocks], factor[:, blocks], root[:, blocks], ALU.mult)
 
-        def capsules(a_ps, factor, kb, cap_t):
+        def capsules(a_ps, factor, kb, cap_t, on_vector):
             cap = two.tile([P, F], BF16, name="cap")
-            nc.vector.tensor_scalar_mul(cap[:], a_ps[:, kb * F : (kb + 1) * F], factor[:, kb : kb + 1])
             cap_ps = psum_h.tile([F, P], BF16, name="cap_ps", tag="h")
-            nc.tensor.transpose(cap_ps[:], cap[:], ident_b[:])
-            nc.vector.tensor_copy(cap_t, cap_ps[:])
+            if on_vector:
+                nc.vector.tensor_scalar_mul(cap[:], a_ps[:, kb * F : (kb + 1) * F], factor[:, kb : kb + 1])
+                nc.tensor.transpose(cap_ps[:], cap[:], ident_b[:])
+                nc.vector.tensor_copy(cap_t, cap_ps[:])
+            else:
+                nc.scalar.activation(cap[:], a_ps[:, kb * F : (kb + 1) * F], FN.Copy, scale=factor[:, kb : kb + 1])
+                nc.tensor.transpose(cap_ps[:], cap[:], ident_b[:])
+                nc.scalar.copy(cap_t, cap_ps[:])
 
         a0_ps = psum_a.tile([P, K], F32, name="a0_ps", tag="a")
         with tc.tile_pool(name="adj", bufs=NCH) as adj_pool:
@@ -201,25 +213,20 @@ def tile_routingassignment_b_kernel(tc, base, x, adj_t, w, b, offs, out):
             def divide(hc):
                 divide_and_sum(pairs[hc], exps, a0_ps)
 
-            stages = [
-                (linear, 1),
-                (aggregate, 2),
-                (add_bias, 0),
-                (gains, -1),
-                (sums_of_squares, 0),
-                (inverse_sums, -2),
-                (relu, 0),
-                (divide, -2),
-                (statistics, 0),
-                (shifts, -1),
-                (exponentials, -1),
-                (round_h, 2),
-                (mean_and_variance, 0),
-            ]
             for turn in range(-2, NH + 2):
-                for stage, ahead in stages:
-                    if 0 <= turn + ahead < NH:
-                        stage(turn + ahead)
+                run(linear, turn + 1)
+                run(aggregate, turn + 2)
+                run(add_bias, turn)
+                run(gains, turn - 1)
+                run(sums_of_squares, turn)
+                run(inverse_sums, turn - 2)
+                run(relu, turn)
+                run(divide, turn - 2)
+                run(statistics, turn)
+                run(shifts, turn - 1)
+                run(exponentials, turn - 1)
+                run(round_h, turn + 2)
+                run(mean_and_variance, turn)
 
         for c in range(NCH):
             x_ps = psum_w.tile([F, CH], BF16, name="x_ps", tag="w")
@@ -233,10 +240,13 @@ def tile_routingassignment_b_kernel(tc, base, x, adj_t, w, b, offs, out):
             nc.sync.dma_start(windows[kb][:], base[kb * P : (kb + 1) * P, :])
         s1_t = [late.tile([P, N], F32, name=f"s1_t{kb}") for kb in range(KB)]
 
-        factor0 = squash_factor(a0_ps)
+        q0 = held.tile([P, KB], F32, name="q0")
+        factor0 = held.tile([P, KB], F32, name="factor0")
+        squash_factor(a0_ps, q0, factor0, 0, KB // 2)
+        squash_factor(a0_ps, q0, factor0, KB // 2, KB)
         cap0_t = held.tile([F, K], BF16, name="cap0_t")
         for kb in range(KB):
-            capsules(a0_ps, factor0, kb, cap0_t[:, kb * P : (kb + 1) * P])
+            capsules(a0_ps, factor0, kb, cap0_t[:, kb * P : (kb + 1) * P], on_vector=True)
 
         def transpose_s1(kb, c):
             turned = psum_h.tile([P, CH], F32, name="turned", tag="h")
@@ -268,11 +278,14 @@ def tile_routingassignment_b_kernel(tc, base, x, adj_t, w, b, offs, out):
                 nc.vector.reciprocal(inverse[:, nb : nb + 1], total[:, nb : nb + 1])
                 divide_and_sum((nb,), exps, a1_ps)
             transpose_s1(0, c)
-        factor1 = squash_factor(a1_ps)
 
+        q1 = held.tile([P, KB], F32, name="q1")
+        factor1 = held.tile([P, KB], F32, name="factor1")
+        squash_factor(a1_ps, q1, factor1, 0, 1)
+        squash_factor(a1_ps, q1, factor1, 1, KB)
         for kb in range(KB):
             cap1_t = two.tile([F, P], BF16, name="cap1_t")
-            capsules(a1_ps, factor1, kb, cap1_t[:])
+            capsules(a1_ps, factor1, kb, cap1_t[:], on_vector=(kb == 0))
             if kb > 0:
                 for c in range(NCH):
                     transpose_s1(kb, c)
@@ -283,6 +296,9 @@ def tile_routingassignment_b_kernel(tc, base, x, adj_t, w, b, offs, out):
                     last_ps[:], lhsT=cap1_t[:], rhs=x_t[:, c * CH : (c + 1) * CH],
                     start=True, stop=True,
                 )
-                nc.scalar.copy(last_step[:, c * CH : (c + 1) * CH], last_ps[:])
+                if kb == 0 and c % 2 == 1:
+                    nc.vector.tensor_copy(last_step[:, c * CH : (c + 1) * CH], last_ps[:])
+                else:
+                    nc.scalar.copy(last_step[:, c * CH : (c + 1) * CH], last_ps[:])
             nc.vector.tensor_tensor(windows[kb][:].indirect(offsets[:]), s1_t[kb][:], last_step[:], ALU.add)
             nc.sync.dma_start(out[kb * P : (kb + 1) * P, :], windows[kb][:])

@@ -20,6 +20,7 @@ BPC = CH // P
 HALF = CH // 2
 NH = N // HALF
 BPH = HALF // P
+EARLY = 5
 BN_EPS = 1e-5
 NORM_EPS = 1e-12
 
@@ -33,8 +34,6 @@ def tile_routingassignment_b_kernel(tc, base, x, adj_t, w, b, offs, out):
         two = ctx.enter_context(tc.tile_pool(name="two", bufs=2))
         four = ctx.enter_context(tc.tile_pool(name="four", bufs=4))
         psum_a = ctx.enter_context(tc.psum_pool(name="psum_a", bufs=1))
-        psum_h = ctx.enter_context(tc.psum_pool(name="psum_h", bufs=3))
-        psum_w = ctx.enter_context(tc.psum_pool(name="psum_w", bufs=4))
 
         b_row = held.tile([1, K], F32, name="b_row")
         nc.scalar.dma_start(b_row[:], b.rearrange("k one -> one k"))
@@ -54,13 +53,6 @@ def tile_routingassignment_b_kernel(tc, base, x, adj_t, w, b, offs, out):
         nc.vector.memset(minus_half[:], -0.5)
         plus_half = held.tile([P, KB], F32, name="plus_half")
         nc.vector.memset(plus_half[:], 0.5)
-
-        ones_row = held.tile([1, P], F32, name="ones_row")
-        nc.vector.memset(ones_row[:], 1.0)
-        b_ps = psum_w.tile([P, K], F32, name="b_ps", tag="w")
-        nc.tensor.matmul(b_ps[:], lhsT=ones_row[:], rhs=b_row[:], start=True, stop=True)
-        b_all = held.tile([P, K], F32, name="b_all")
-        nc.vector.tensor_copy(b_all[:], b_ps[:])
 
         ssq = held.tile([P, NB], F32, name="ssq")
         stats = held.tile([P, NB, 6], F32, name="stats")
@@ -114,9 +106,121 @@ def tile_routingassignment_b_kernel(tc, base, x, adj_t, w, b, offs, out):
             nc.vector.reciprocal(factor[:, blocks], factor[:, blocks])
             nc.vector.tensor_tensor(factor[:, blocks], factor[:, blocks], root[:, blocks], ALU.mult)
 
+        a0_ps = psum_a.tile([P, K], F32, name="a0_ps", tag="a")
+        with tc.psum_pool(name="psum_h", bufs=3) as psum_h, tc.psum_pool(name="psum_u", bufs=4) as psum_u:
+            ones_row = held.tile([1, P], F32, name="ones_row")
+            nc.vector.memset(ones_row[:], 1.0)
+            b_ps = psum_u.tile([P, K], F32, name="b_ps", tag="u")
+            nc.tensor.matmul(b_ps[:], lhsT=ones_row[:], rhs=b_row[:], start=True, stop=True)
+            b_all = held.tile([P, K], F32, name="b_all")
+            nc.vector.tensor_copy(b_all[:], b_ps[:])
+
+            with tc.tile_pool(name="adj", bufs=NCH) as adj_pool:
+                adj_runs = adj_t.rearrange("(t p) j -> p t j", p=P)
+                adj_chunks = []
+                for c in range(NCH):
+                    adj_c = adj_pool.tile([P, NB, CH], BF16, name="adj_c")
+                    parts = [(0, HALF), (HALF, CH)] if c == 0 else [(0, CH)]
+                    rows = BPC * len(parts)
+                    for lo, hi in parts:
+                        for q in range(0, NB, rows):
+                            nc.sync.dma_start(adj_c[:, q : q + rows, lo:hi], adj_runs[:, q : q + rows, c * CH + lo : c * CH + hi])
+                    adj_chunks.append(adj_c)
+                nc.sync.dma_start(offsets[:], offs)
+
+                h_pss, h_bfs, u_pss, us, exps = {}, {}, {}, {}, {}
+
+                def aggregate(hc):
+                    adj_half = adj_chunks[hc // 2][:, :, (hc % 2) * HALF : (hc % 2 + 1) * HALF]
+                    h_pss[hc] = psum_h.tile([F, HALF], F32, name="h_ps", tag="h")
+                    for t in range(NB):
+                        nc.tensor.matmul(
+                            h_pss[hc][:], lhsT=x_sb[:, t, :], rhs=adj_half[:, t, :], start=(t == 0), stop=(t == NB - 1)
+                        )
+
+                def round_h(hc):
+                    h_bfs[hc] = four.tile([F, HALF], BF16, name="h_bf")
+                    nc.scalar.copy(h_bfs[hc][:], h_pss[hc][:])
+
+                def linear(hc):
+                    for r, nb in enumerate(pairs[hc]):
+                        u_pss[nb] = psum_u.tile([P, K], F32, name="u_ps", tag="u")
+                        nc.tensor.matmul(
+                            u_pss[nb][:], lhsT=h_bfs[hc][:, r * P : (r + 1) * P], rhs=w_sb[:], start=True, stop=True
+                        )
+
+                def add_bias(hc):
+                    for nb in pairs[hc]:
+                        us[nb] = four.tile([P, K], F32, name="u")
+                        nc.vector.tensor_tensor(us[nb][:], u_pss[nb][:], b_all[:], ALU.add)
+
+                def sums_of_squares(hc):
+                    for nb in pairs[hc]:
+                        squares = four.tile([P, K], BF16, name="squares")
+                        nc.scalar.activation(
+                            squares[:], us[nb][:], FN.Square, scale=math.sqrt(BN_EPS), accum_out=ssq[:, nb : nb + 1]
+                        )
+
+                def relu(hc):
+                    for nb in pairs[hc]:
+                        nc.vector.tensor_scalar_max(logits[nb][:], us[nb][:], 0.0)
+
+                def statistics(hc):
+                    for nb in pairs[hc]:
+                        nc.vector.bn_stats(stats[:, nb, :], logits[nb][:])
+
+                def mean_and_variance(hc):
+                    for nb in pairs[hc]:
+                        nc.vector.bn_aggr(mean_var[:, nb, :], stats[:, nb, :])
+
+                def gains(hc):
+                    blocks = columns(pairs[hc])
+                    nc.vector.scalar_tensor_tensor(
+                        spread[:, blocks], ssq[:, blocks], BN_EPS * NORM_EPS * NORM_EPS, mean_var[:, blocks, 1],
+                        ALU.max, ALU.add,
+                    )
+                    nc.gpsimd.tensor_tensor(gain[:, blocks], spread[:, blocks], minus_half[:], ALU.pow)
+
+                def shifts(hc):
+                    blocks = columns(pairs[hc])
+                    nc.vector.scalar_tensor_tensor(
+                        shift[:, blocks], mean_var[:, blocks, 0], -1.0, gain[:, blocks], ALU.mult, ALU.mult
+                    )
+
+                def exponentials(hc):
+                    for nb in pairs[hc]:
+                        exps[nb] = four.tile([P, K], F32, name="e")
+                        nc.scalar.activation(
+                            exps[nb][:], logits[nb][:], FN.Exp, bias=shift[:, nb : nb + 1], scale=gain[:, nb : nb + 1],
+                            accum_out=total[:, nb : nb + 1],
+                        )
+
+                def inverse_sums(hc):
+                    nc.vector.reciprocal(inverse[:, columns(pairs[hc])], total[:, columns(pairs[hc])])
+
+                def divide(hc):
+                    divide_and_sum(pairs[hc], exps, a0_ps)
+
+                for turn in range(-2, NH + 2):
+                    run(linear, turn + 1)
+                    run(aggregate, turn + 2)
+                    run(add_bias, turn)
+                    run(gains, turn - 1)
+                    run(sums_of_squares, turn)
+                    run(inverse_sums, turn - 2)
+                    run(relu, turn)
+                    run(divide, turn - 2)
+                    run(statistics, turn)
+                    run(shifts, turn - 1)
+                    run(exponentials, turn - 1)
+                    run(round_h, turn + 2)
+                    run(mean_and_variance, turn)
+
+        psum_r = ctx.enter_context(tc.psum_pool(name="psum_r", bufs=7))
+
         def capsules(a_ps, factor, kb, cap_t, on_vector):
             cap = two.tile([P, F], BF16, name="cap")
-            cap_ps = psum_h.tile([F, P], BF16, name="cap_ps", tag="h")
+            cap_ps = psum_r.tile([F, P], BF16, name="cap_ps", tag="r")
             if on_vector:
                 nc.vector.tensor_scalar_mul(cap[:], a_ps[:, kb * F : (kb + 1) * F], factor[:, kb : kb + 1])
                 nc.tensor.transpose(cap_ps[:], cap[:], ident_b[:])
@@ -126,110 +230,8 @@ def tile_routingassignment_b_kernel(tc, base, x, adj_t, w, b, offs, out):
                 nc.tensor.transpose(cap_ps[:], cap[:], ident_b[:])
                 nc.scalar.copy(cap_t, cap_ps[:])
 
-        a0_ps = psum_a.tile([P, K], F32, name="a0_ps", tag="a")
-        with tc.tile_pool(name="adj", bufs=NCH) as adj_pool:
-            adj_runs = adj_t.rearrange("(t p) j -> p t j", p=P)
-            adj_chunks = []
-            for c in range(NCH):
-                adj_c = adj_pool.tile([P, NB, CH], BF16, name="adj_c")
-                parts = [(0, HALF), (HALF, CH)] if c == 0 else [(0, CH)]
-                rows = BPC * len(parts)
-                for lo, hi in parts:
-                    for q in range(0, NB, rows):
-                        nc.sync.dma_start(adj_c[:, q : q + rows, lo:hi], adj_runs[:, q : q + rows, c * CH + lo : c * CH + hi])
-                adj_chunks.append(adj_c)
-            nc.sync.dma_start(offsets[:], offs)
-
-            h_pss, h_bfs, u_pss, us, exps = {}, {}, {}, {}, {}
-
-            def aggregate(hc):
-                adj_half = adj_chunks[hc // 2][:, :, (hc % 2) * HALF : (hc % 2 + 1) * HALF]
-                h_pss[hc] = psum_h.tile([F, HALF], F32, name="h_ps", tag="h")
-                for t in range(NB):
-                    nc.tensor.matmul(
-                        h_pss[hc][:], lhsT=x_sb[:, t, :], rhs=adj_half[:, t, :], start=(t == 0), stop=(t == NB - 1)
-                    )
-
-            def round_h(hc):
-                h_bfs[hc] = four.tile([F, HALF], BF16, name="h_bf")
-                nc.scalar.copy(h_bfs[hc][:], h_pss[hc][:])
-
-            def linear(hc):
-                for r, nb in enumerate(pairs[hc]):
-                    u_pss[nb] = psum_w.tile([P, K], F32, name="u_ps", tag="w")
-                    nc.tensor.matmul(
-                        u_pss[nb][:], lhsT=h_bfs[hc][:, r * P : (r + 1) * P], rhs=w_sb[:], start=True, stop=True
-                    )
-
-            def add_bias(hc):
-                for nb in pairs[hc]:
-                    us[nb] = four.tile([P, K], F32, name="u")
-                    nc.vector.tensor_tensor(us[nb][:], u_pss[nb][:], b_all[:], ALU.add)
-
-            def sums_of_squares(hc):
-                for nb in pairs[hc]:
-                    squares = four.tile([P, K], BF16, name="squares")
-                    nc.scalar.activation(
-                        squares[:], us[nb][:], FN.Square, scale=math.sqrt(BN_EPS), accum_out=ssq[:, nb : nb + 1]
-                    )
-
-            def relu(hc):
-                for nb in pairs[hc]:
-                    nc.vector.tensor_scalar_max(logits[nb][:], us[nb][:], 0.0)
-
-            def statistics(hc):
-                for nb in pairs[hc]:
-                    nc.vector.bn_stats(stats[:, nb, :], logits[nb][:])
-
-            def mean_and_variance(hc):
-                for nb in pairs[hc]:
-                    nc.vector.bn_aggr(mean_var[:, nb, :], stats[:, nb, :])
-
-            def gains(hc):
-                blocks = columns(pairs[hc])
-                nc.vector.scalar_tensor_tensor(
-                    spread[:, blocks], ssq[:, blocks], BN_EPS * NORM_EPS * NORM_EPS, mean_var[:, blocks, 1],
-                    ALU.max, ALU.add,
-                )
-                nc.gpsimd.tensor_tensor(gain[:, blocks], spread[:, blocks], minus_half[:], ALU.pow)
-
-            def shifts(hc):
-                blocks = columns(pairs[hc])
-                nc.vector.scalar_tensor_tensor(
-                    shift[:, blocks], mean_var[:, blocks, 0], -1.0, gain[:, blocks], ALU.mult, ALU.mult
-                )
-
-            def exponentials(hc):
-                for nb in pairs[hc]:
-                    exps[nb] = four.tile([P, K], F32, name="e")
-                    nc.scalar.activation(
-                        exps[nb][:], logits[nb][:], FN.Exp, bias=shift[:, nb : nb + 1], scale=gain[:, nb : nb + 1],
-                        accum_out=total[:, nb : nb + 1],
-                    )
-
-            def inverse_sums(hc):
-                nc.vector.reciprocal(inverse[:, columns(pairs[hc])], total[:, columns(pairs[hc])])
-
-            def divide(hc):
-                divide_and_sum(pairs[hc], exps, a0_ps)
-
-            for turn in range(-2, NH + 2):
-                run(linear, turn + 1)
-                run(aggregate, turn + 2)
-                run(add_bias, turn)
-                run(gains, turn - 1)
-                run(sums_of_squares, turn)
-                run(inverse_sums, turn - 2)
-                run(relu, turn)
-                run(divide, turn - 2)
-                run(statistics, turn)
-                run(shifts, turn - 1)
-                run(exponentials, turn - 1)
-                run(round_h, turn + 2)
-                run(mean_and_variance, turn)
-
         for c in range(NCH):
-            x_ps = psum_w.tile([F, CH], BF16, name="x_ps", tag="w")
+            x_ps = psum_r.tile([F, CH], BF16, name="x_ps", tag="r")
             for r in range(BPC):
                 nc.tensor.transpose(x_ps[:, r * P : (r + 1) * P], x_sb[:, c * BPC + r, :], ident_b[:])
             nc.vector.tensor_copy(x_t[:, c * CH : (c + 1) * CH], x_ps[:])
@@ -240,6 +242,14 @@ def tile_routingassignment_b_kernel(tc, base, x, adj_t, w, b, offs, out):
             nc.sync.dma_start(windows[kb][:], base[kb * P : (kb + 1) * P, :])
         s1_t = [late.tile([P, N], F32, name=f"s1_t{kb}") for kb in range(KB)]
 
+        early_ps = {}
+        for nb in range(EARLY):
+            nc.vector.tensor_scalar(
+                logits[nb][:], logits[nb][:], gain[:, nb : nb + 1], shift[:, nb : nb + 1], ALU.mult, ALU.add
+            )
+            early_ps[nb] = psum_r.tile([P, K], F32, name="step_ps", tag="r")
+            nc.tensor.matmul(early_ps[nb][:], lhsT=ident_f[:], rhs=logits[nb][:], start=True, stop=False)
+
         q0 = held.tile([P, KB], F32, name="q0")
         factor0 = held.tile([P, KB], F32, name="factor0")
         squash_factor(a0_ps, q0, factor0, 0, KB // 2)
@@ -249,7 +259,7 @@ def tile_routingassignment_b_kernel(tc, base, x, adj_t, w, b, offs, out):
             capsules(a0_ps, factor0, kb, cap0_t[:, kb * P : (kb + 1) * P], on_vector=True)
 
         def transpose_s1(kb, c):
-            turned = psum_h.tile([P, CH], F32, name="turned", tag="h")
+            turned = psum_r.tile([P, CH], F32, name="turned", tag="r")
             for r in range(BPC):
                 nc.tensor.transpose(
                     turned[:, r * P : (r + 1) * P], logits[c * BPC + r][:, kb * P : (kb + 1) * P], ident_f[:]
@@ -259,16 +269,26 @@ def tile_routingassignment_b_kernel(tc, base, x, adj_t, w, b, offs, out):
         a1_ps = psum_a.tile([P, K], F32, name="a1_ps", tag="a")
         for c in range(NCH):
             for nb in range(c * BPC, (c + 1) * BPC):
-                step_ps = psum_w.tile([P, K], F32, name="step_ps", tag="w")
-                nc.tensor.matmul(step_ps[:], lhsT=x_t[:, nb * P : (nb + 1) * P], rhs=cap0_t[:], start=True, stop=True)
-                partial = four.tile([P, K], F32, name="partial")
-                nc.vector.scalar_tensor_tensor(
-                    partial[:], logits[nb][:], gain[:, nb : nb + 1], step_ps[:], ALU.mult, ALU.add
-                )
-                nc.vector.tensor_scalar(
-                    logits[nb][:], partial[:], shift[:, nb : nb + 1], None, ALU.add, ALU.max,
-                    accum_out=top[:, nb : nb + 1],
-                )
+                if nb < EARLY:
+                    nc.tensor.matmul(
+                        early_ps[nb][:], lhsT=x_t[:, nb * P : (nb + 1) * P], rhs=cap0_t[:], start=False, stop=True
+                    )
+                    nc.vector.tensor_scalar(
+                        logits[nb][:], early_ps[nb][:], 0.0, None, ALU.add, ALU.max, accum_out=top[:, nb : nb + 1]
+                    )
+                else:
+                    step_ps = psum_r.tile([P, K], F32, name="step_ps", tag="r")
+                    nc.tensor.matmul(
+                        step_ps[:], lhsT=x_t[:, nb * P : (nb + 1) * P], rhs=cap0_t[:], start=True, stop=True
+                    )
+                    partial = four.tile([P, K], F32, name="partial")
+                    nc.vector.scalar_tensor_tensor(
+                        partial[:], logits[nb][:], gain[:, nb : nb + 1], step_ps[:], ALU.mult, ALU.add
+                    )
+                    nc.vector.tensor_scalar(
+                        logits[nb][:], partial[:], shift[:, nb : nb + 1], None, ALU.add, ALU.max,
+                        accum_out=top[:, nb : nb + 1],
+                    )
                 nc.scalar.mul(minus_top[:, nb : nb + 1], top[:, nb : nb + 1], -1.0)
                 exps[nb] = four.tile([P, K], F32, name="e")
                 nc.scalar.activation(
@@ -291,7 +311,7 @@ def tile_routingassignment_b_kernel(tc, base, x, adj_t, w, b, offs, out):
                     transpose_s1(kb, c)
             last_step = late.tile([P, N], F32, name="last_step", bufs=2)
             for c in range(NCH):
-                last_ps = psum_w.tile([P, CH], F32, name="last_ps", tag="w")
+                last_ps = psum_r.tile([P, CH], F32, name="last_ps", tag="r")
                 nc.tensor.matmul(
                     last_ps[:], lhsT=cap1_t[:], rhs=x_t[:, c * CH : (c + 1) * CH],
                     start=True, stop=True,

@@ -297,6 +297,7 @@ def tile_routingassignment_b_kernel(tc, base, x, adj_t, w, b, offs, out):
                 )
                 nc.vector.reciprocal(inverse[:, nb : nb + 1], total[:, nb : nb + 1])
                 divide_and_sum((nb,), exps, a1_ps)
+        for c in range(NCH):
             transpose_s1(0, c)
 
         q1 = held.tile([P, KB], F32, name="q1")

@@ -20,7 +20,7 @@ BPC = CH // P
 HALF = CH // 2
 NH = N // HALF
 BPH = HALF // P
-EARLY = 5
+EARLY = 6
 BN_EPS = 1e-5
 NORM_EPS = 1e-12
 
@@ -60,7 +60,6 @@ def tile_routingassignment_b_kernel(tc, base, x, adj_t, w, b, offs, out):
         spread = held.tile([P, NB], F32, name="spread")
         gain = held.tile([P, NB], F32, name="gain")
         shift = held.tile([P, NB], F32, name="shift")
-        top = held.tile([P, NB], F32, name="top")
         minus_top = held.tile([P, NB], F32, name="minus_top")
         total = held.tile([P, NB], F32, name="total")
         inverse = held.tile([P, NB], F32, name="inverse")
@@ -93,18 +92,16 @@ def tile_routingassignment_b_kernel(tc, base, x, adj_t, w, b, offs, out):
                         stop=(nb == NB - 1 and kb == KB - 1),
                     )
 
-        def squash_factor(a_ps, q, factor, first, last):
+        def squash_factor(a_ps, q, root, inverse_of, first, last):
             blocks = slice(first, last)
             for kb in range(first, last):
                 a_squares = two.tile([P, F], BF16, name="a_squares")
                 nc.scalar.activation(
                     a_squares[:], a_ps[:, kb * F : (kb + 1) * F], FN.Square, accum_out=q[:, kb : kb + 1]
                 )
-            root = two.tile([P, KB], F32, name="root")
             nc.gpsimd.tensor_tensor(root[:, blocks], q[:, blocks], plus_half[:, blocks], ALU.pow)
-            nc.vector.tensor_scalar_add(factor[:, blocks], q[:, blocks], 1.0)
-            nc.vector.reciprocal(factor[:, blocks], factor[:, blocks])
-            nc.vector.tensor_tensor(factor[:, blocks], factor[:, blocks], root[:, blocks], ALU.mult)
+            nc.vector.tensor_scalar_add(inverse_of[:, blocks], q[:, blocks], 1.0)
+            nc.vector.reciprocal(inverse_of[:, blocks], inverse_of[:, blocks])
 
         a0_ps = psum_a.tile([P, K], F32, name="a0_ps", tag="a")
         with tc.psum_pool(name="psum_h", bufs=3) as psum_h, tc.psum_pool(name="psum_u", bufs=4) as psum_u:
@@ -218,15 +215,20 @@ def tile_routingassignment_b_kernel(tc, base, x, adj_t, w, b, offs, out):
 
         psum_r = ctx.enter_context(tc.psum_pool(name="psum_r", bufs=7))
 
-        def capsules(a_ps, factor, kb, cap_t, on_vector):
+        def capsules(a_ps, root, inverse_of, kb, cap_t, on_vector):
             cap = two.tile([P, F], BF16, name="cap")
             cap_ps = psum_r.tile([F, P], BF16, name="cap_ps", tag="r")
             if on_vector:
-                nc.vector.tensor_scalar_mul(cap[:], a_ps[:, kb * F : (kb + 1) * F], factor[:, kb : kb + 1])
+                nc.vector.tensor_scalar(
+                    cap[:], a_ps[:, kb * F : (kb + 1) * F], root[:, kb : kb + 1], inverse_of[:, kb : kb + 1],
+                    ALU.mult, ALU.mult,
+                )
                 nc.tensor.transpose(cap_ps[:], cap[:], ident_b[:])
                 nc.vector.tensor_copy(cap_t, cap_ps[:])
             else:
-                nc.scalar.activation(cap[:], a_ps[:, kb * F : (kb + 1) * F], FN.Copy, scale=factor[:, kb : kb + 1])
+                scaled = two.tile([P, F], F32, name="scaled")
+                nc.scalar.activation(scaled[:], a_ps[:, kb * F : (kb + 1) * F], FN.Copy, scale=root[:, kb : kb + 1])
+                nc.scalar.activation(cap[:], scaled[:], FN.Copy, scale=inverse_of[:, kb : kb + 1])
                 nc.tensor.transpose(cap_ps[:], cap[:], ident_b[:])
                 nc.scalar.copy(cap_t, cap_ps[:])
 
@@ -251,12 +253,22 @@ def tile_routingassignment_b_kernel(tc, base, x, adj_t, w, b, offs, out):
             nc.tensor.matmul(early_ps[nb][:], lhsT=ident_f[:], rhs=logits[nb][:], start=True, stop=False)
 
         q0 = held.tile([P, KB], F32, name="q0")
-        factor0 = held.tile([P, KB], F32, name="factor0")
-        squash_factor(a0_ps, q0, factor0, 0, KB // 2)
-        squash_factor(a0_ps, q0, factor0, KB // 2, KB)
+        root0 = held.tile([P, KB], F32, name="root0")
+        inverse_of0 = held.tile([P, KB], F32, name="inverse_of0")
+        squash_factor(a0_ps, q0, root0, inverse_of0, 0, KB // 2)
+        squash_factor(a0_ps, q0, root0, inverse_of0, KB // 2, KB)
         cap0_t = held.tile([F, K], BF16, name="cap0_t")
+        cap0_ps = psum_r.tile([F, K], BF16, name="cap0_ps", tag="r")
         for kb in range(KB):
-            capsules(a0_ps, factor0, kb, cap0_t[:, kb * P : (kb + 1) * P], on_vector=True)
+            cap0 = four.tile([P, F], BF16, name="cap0")
+            nc.vector.tensor_scalar(
+                cap0[:], a0_ps[:, kb * F : (kb + 1) * F], root0[:, kb : kb + 1], inverse_of0[:, kb : kb + 1],
+                ALU.mult, ALU.mult,
+            )
+            nc.tensor.transpose(cap0_ps[:, kb * P : (kb + 1) * P], cap0[:], ident_b[:])
+        nc.vector.tensor_copy(cap0_t[:], cap0_ps[:])
+        minus_gain = held.tile([P, NB], F32, name="minus_gain")
+        nc.vector.tensor_scalar_mul(minus_gain[:], gain[:], -1.0)
 
         def transpose_s1(kb, c):
             turned = psum_r.tile([P, CH], F32, name="turned", tag="r")
@@ -264,7 +276,7 @@ def tile_routingassignment_b_kernel(tc, base, x, adj_t, w, b, offs, out):
                 nc.tensor.transpose(
                     turned[:, r * P : (r + 1) * P], logits[c * BPC + r][:, kb * P : (kb + 1) * P], ident_f[:]
                 )
-            nc.scalar.copy(s1_t[kb][:, c * CH : (c + 1) * CH], turned[:])
+            nc.scalar.mul(s1_t[kb][:, c * CH : (c + 1) * CH], turned[:], -1.0)
 
         a1_ps = psum_a.tile([P, K], F32, name="a1_ps", tag="a")
         for c in range(NCH):
@@ -274,7 +286,7 @@ def tile_routingassignment_b_kernel(tc, base, x, adj_t, w, b, offs, out):
                         early_ps[nb][:], lhsT=x_t[:, nb * P : (nb + 1) * P], rhs=cap0_t[:], start=False, stop=True
                     )
                     nc.vector.tensor_scalar(
-                        logits[nb][:], early_ps[nb][:], 0.0, None, ALU.add, ALU.max, accum_out=top[:, nb : nb + 1]
+                        logits[nb][:], early_ps[nb][:], -1.0, None, ALU.mult, ALU.min, accum_out=minus_top[:, nb : nb + 1]
                     )
                 else:
                     step_ps = psum_r.tile([P, K], F32, name="step_ps", tag="r")
@@ -283,16 +295,15 @@ def tile_routingassignment_b_kernel(tc, base, x, adj_t, w, b, offs, out):
                     )
                     partial = four.tile([P, K], F32, name="partial")
                     nc.vector.scalar_tensor_tensor(
-                        partial[:], logits[nb][:], gain[:, nb : nb + 1], step_ps[:], ALU.mult, ALU.add
+                        partial[:], logits[nb][:], minus_gain[:, nb : nb + 1], step_ps[:], ALU.mult, ALU.subtract
                     )
                     nc.vector.tensor_scalar(
-                        logits[nb][:], partial[:], shift[:, nb : nb + 1], None, ALU.add, ALU.max,
-                        accum_out=top[:, nb : nb + 1],
+                        logits[nb][:], partial[:], shift[:, nb : nb + 1], None, ALU.subtract, ALU.min,
+                        accum_out=minus_top[:, nb : nb + 1],
                     )
-                nc.scalar.mul(minus_top[:, nb : nb + 1], top[:, nb : nb + 1], -1.0)
                 exps[nb] = four.tile([P, K], F32, name="e")
                 nc.scalar.activation(
-                    exps[nb][:], logits[nb][:], FN.Exp, bias=minus_top[:, nb : nb + 1], scale=1.0,
+                    exps[nb][:], logits[nb][:], FN.Exp, bias=minus_top[:, nb : nb + 1], scale=-1.0,
                     accum_out=total[:, nb : nb + 1],
                 )
                 nc.vector.reciprocal(inverse[:, nb : nb + 1], total[:, nb : nb + 1])
@@ -301,12 +312,13 @@ def tile_routingassignment_b_kernel(tc, base, x, adj_t, w, b, offs, out):
             transpose_s1(0, c)
 
         q1 = held.tile([P, KB], F32, name="q1")
-        factor1 = held.tile([P, KB], F32, name="factor1")
-        squash_factor(a1_ps, q1, factor1, 0, 1)
-        squash_factor(a1_ps, q1, factor1, 1, KB)
+        root1 = held.tile([P, KB], F32, name="root1")
+        inverse_of1 = held.tile([P, KB], F32, name="inverse_of1")
+        squash_factor(a1_ps, q1, root1, inverse_of1, 0, 1)
+        squash_factor(a1_ps, q1, root1, inverse_of1, 1, KB)
         for kb in range(KB):
             cap1_t = two.tile([F, P], BF16, name="cap1_t")
-            capsules(a1_ps, factor1, kb, cap1_t[:], on_vector=(kb == 0))
+            capsules(a1_ps, root1, inverse_of1, kb, cap1_t[:], on_vector=(kb == 0))
             if kb > 0:
                 for c in range(NCH):
                     transpose_s1(kb, c)

@@ -35,12 +35,10 @@ def tile_routingassignment_b_kernel(tc, base, x, adj_t, w, b, offs, out):
         four = ctx.enter_context(tc.tile_pool(name="four", bufs=4))
         psum_a = ctx.enter_context(tc.psum_pool(name="psum_a", bufs=1))
 
-        b_row = held.tile([1, K], F32, name="b_row")
-        nc.scalar.dma_start(b_row[:], b.rearrange("k one -> one k"))
         x_sb = held.tile([P, NB, F], BF16, name="x_sb")
         x_blocks = x.rearrange("(nb p) f -> p nb f", p=P)
-        for lo in (0, NB // 2):
-            nc.scalar.dma_start(x_sb[:, lo : lo + NB // 2, :], x_blocks[:, lo : lo + NB // 2, :])
+        for lo in range(0, NB, BPC):
+            nc.scalar.dma_start(x_sb[:, lo : lo + BPC, :], x_blocks[:, lo : lo + BPC, :])
         w_sb = held.tile([F, K], BF16, name="w_sb")
         nc.scalar.dma_start(w_sb[:], w)
         offsets = held.tile([P, N // 16], U16, name="offsets")
@@ -105,23 +103,18 @@ def tile_routingassignment_b_kernel(tc, base, x, adj_t, w, b, offs, out):
 
         a0_ps = psum_a.tile([P, K], F32, name="a0_ps", tag="a")
         with tc.psum_pool(name="psum_h", bufs=3) as psum_h, tc.psum_pool(name="psum_u", bufs=4) as psum_u:
-            ones_row = held.tile([1, P], F32, name="ones_row")
-            nc.vector.memset(ones_row[:], 1.0)
-            b_ps = psum_u.tile([P, K], F32, name="b_ps", tag="u")
-            nc.tensor.matmul(b_ps[:], lhsT=ones_row[:], rhs=b_row[:], start=True, stop=True)
             b_all = held.tile([P, K], F32, name="b_all")
-            nc.vector.tensor_copy(b_all[:], b_ps[:])
-
             with tc.tile_pool(name="adj", bufs=NCH) as adj_pool:
                 adj_runs = adj_t.rearrange("(t p) j -> p t j", p=P)
                 adj_chunks = []
                 for c in range(NCH):
                     adj_c = adj_pool.tile([P, NB, CH], BF16, name="adj_c")
                     parts = [(0, HALF), (HALF, CH)] if c == 0 else [(0, CH)]
-                    rows = BPC * len(parts)
                     for lo, hi in parts:
-                        for q in range(0, NB, rows):
-                            nc.sync.dma_start(adj_c[:, q : q + rows, lo:hi], adj_runs[:, q : q + rows, c * CH + lo : c * CH + hi])
+                        for q in range(0, NB, BPC):
+                            nc.sync.dma_start(adj_c[:, q : q + BPC, lo:hi], adj_runs[:, q : q + BPC, c * CH + lo : c * CH + hi])
+                        if c == 0 and lo == 0:
+                            nc.sync.dma_start(b_all[:], b.rearrange("k one -> (k one)").partition_broadcast(P))
                     adj_chunks.append(adj_c)
                 nc.sync.dma_start(offsets[:], offs)
 

@@ -90,14 +90,17 @@ def tile_routingassignment_b_kernel(tc, base, x, adj_t, w, b, offs, out):
                         stop=(nb == NB - 1 and kb == KB - 1),
                     )
 
-        def squash_factor(a_ps, q, root, inverse_of, first, last):
+        def squash_factor(a_ps, q, root, inverse_of, first, last, on_scalar):
             blocks = slice(first, last)
             for kb in range(first, last):
                 a_squares = two.tile([P, F], BF16, name="a_squares")
                 nc.scalar.activation(
                     a_squares[:], a_ps[:, kb * F : (kb + 1) * F], FN.Square, accum_out=q[:, kb : kb + 1]
                 )
-            nc.gpsimd.tensor_tensor(root[:, blocks], q[:, blocks], plus_half[:, blocks], ALU.pow)
+            if on_scalar:
+                nc.scalar.activation(root[:, blocks], q[:, blocks], FN.Sqrt)
+            else:
+                nc.gpsimd.tensor_tensor(root[:, blocks], q[:, blocks], plus_half[:, blocks], ALU.pow)
             nc.vector.tensor_scalar_add(inverse_of[:, blocks], q[:, blocks], 1.0)
             nc.vector.reciprocal(inverse_of[:, blocks], inverse_of[:, blocks])
 
@@ -206,6 +209,9 @@ def tile_routingassignment_b_kernel(tc, base, x, adj_t, w, b, offs, out):
                     run(round_h, turn + 2)
                     run(mean_and_variance, turn)
 
+        unread = held.tile([P, 2], F32, name="unread")
+        nc.scalar.activation(unread[:, 0:1], total[:, NB - 1 : NB], FN.Sqrt)
+
         psum_r = ctx.enter_context(tc.psum_pool(name="psum_r", bufs=7))
 
         def capsules(a_ps, root, inverse_of, kb, cap_t, on_vector):
@@ -248,8 +254,8 @@ def tile_routingassignment_b_kernel(tc, base, x, adj_t, w, b, offs, out):
         q0 = held.tile([P, KB], F32, name="q0")
         root0 = held.tile([P, KB], F32, name="root0")
         inverse_of0 = held.tile([P, KB], F32, name="inverse_of0")
-        squash_factor(a0_ps, q0, root0, inverse_of0, 0, KB // 2)
-        squash_factor(a0_ps, q0, root0, inverse_of0, KB // 2, KB)
+        squash_factor(a0_ps, q0, root0, inverse_of0, 0, KB, on_scalar=True)
+        nc.scalar.activation(unread[:, 1:2], root0[:, 0:1], FN.Exp, scale=0.0)
         cap0_t = held.tile([F, K], BF16, name="cap0_t")
         cap0_ps = psum_r.tile([F, K], BF16, name="cap0_ps", tag="r")
         for kb in range(KB):
@@ -307,8 +313,8 @@ def tile_routingassignment_b_kernel(tc, base, x, adj_t, w, b, offs, out):
         q1 = held.tile([P, KB], F32, name="q1")
         root1 = held.tile([P, KB], F32, name="root1")
         inverse_of1 = held.tile([P, KB], F32, name="inverse_of1")
-        squash_factor(a1_ps, q1, root1, inverse_of1, 0, 1)
-        squash_factor(a1_ps, q1, root1, inverse_of1, 1, KB)
+        squash_factor(a1_ps, q1, root1, inverse_of1, 0, 1, on_scalar=False)
+        squash_factor(a1_ps, q1, root1, inverse_of1, 1, KB, on_scalar=False)
         for kb in range(KB):
             cap1_t = two.tile([F, P], BF16, name="cap1_t")
             capsules(a1_ps, root1, inverse_of1, kb, cap1_t[:], on_vector=(kb == 0))

import math
from contextlib import ExitStack

import concourse.mybir as mybir
from concourse.masks import make_identity

F32 = mybir.dt.float32
BF16 = mybir.dt.bfloat16
U16 = mybir.dt.uint16
ALU = mybir.AluOpType
FN = mybir.ActivationFunctionType

P = 128
K, S, N, F = 512, 4096, 2048, 128
NB = N // P
KB = K // P
CH = 512
NCH = N // CH
BPC = CH // P
HALF = CH // 2
NH = N // HALF
BPH = HALF // P
EARLY = 6
BN_EPS = 1e-5
NORM_EPS = 1e-12

FLOPS = 2 * F * N * N + 2 * F * K * N + 2 * (2 * K * N * F + 2 * K * N * F)


def tile_routingassignment_b_kernel(tc, base, x, adj_t, w, b, offs, out):
    nc = tc.nc
    with ExitStack() as ctx:
        held = ctx.enter_context(tc.tile_pool(name="held", bufs=1))
        two = ctx.enter_context(tc.tile_pool(name="two", bufs=2))
        four = ctx.enter_context(tc.tile_pool(name="four", bufs=4))
        psum_a = ctx.enter_context(tc.psum_pool(name="psum_a", bufs=1))

        x_sb = held.tile([P, NB, F], BF16, name="x_sb")
        x_blocks = x.rearrange("(nb p) f -> p nb f", p=P)
        for lo in range(0, NB, BPC):
            nc.scalar.dma_start(x_sb[:, lo : lo + BPC, :], x_blocks[:, lo : lo + BPC, :])
        w_sb = held.tile([F, K], BF16, name="w_sb")
        nc.scalar.dma_start(w_sb[:], w)
        offsets = held.tile([P, N // 16], U16, name="offsets")

        ident_f = held.tile([P, P], F32, name="ident_f")
        make_identity(nc, ident_f[:])
        ident_b = held.tile([P, P], BF16, name="ident_b")
        make_identity(nc, ident_b[:])
        minus_half = held.tile([P, BPH], F32, name="minus_half")
        nc.vector.memset(minus_half[:], -0.5)
        plus_half = held.tile([P, KB], F32, name="plus_half")
        nc.vector.memset(plus_half[:], 0.5)

        ssq = held.tile([P, NB], F32, name="ssq")
        stats = held.tile([P, NB, 6], F32, name="stats")
        mean_var = held.tile([P, NB, 2], F32, name="mean_var")
        spread = held.tile([P, NB], F32, name="spread")
        gain = held.tile([P, NB], F32, name="gain")
        shift = held.tile([P, NB], F32, name="shift")
        minus_top = held.tile([P, NB], F32, name="minus_top")
        total = held.tile([P, NB], F32, name="total")
        inverse = held.tile([P, NB], F32, name="inverse")

        x_t = held.tile([F, N], BF16, name="x_t")
        logits = [held.tile([P, K], F32, name=f"logits{nb}") for nb in range(NB)]

        pairs = [(2 * h, 2 * h + 1) for h in range(NH)]

        def columns(pair):
            return slice(pair[0], pair[1] + 1)

        def run(stage, hc):
            if 0 <= hc < NH:
                stage(hc)

        def divide_and_sum(blocks, exps, a_ps):
            for nb in blocks:
                p = four.tile([P, K], BF16, name="p")
                if nb in pairs[-1]:
                    nc.vector.tensor_scalar_mul(p[:], exps[nb][:], inverse[:, nb : nb + 1])
                else:
                    nc.gpsimd.tensor_scalar(p[:], exps[nb][:], inverse[:, nb : nb + 1], 0.0, ALU.mult, ALU.add)
                for kb in range(KB):
                    nc.tensor.matmul(
                        a_ps[:, kb * F : (kb + 1) * F],
                        lhsT=p[:, kb * P : (kb + 1) * P],
                        rhs=x_sb[:, nb, :],
                        start=(nb == 0 and kb == 0),
                        stop=(nb == NB - 1 and kb == KB - 1),
                    )

        def squash_factor(a_ps, q, root, inverse_of, first, last, on_scalar):
            blocks = slice(first, last)
            for kb in range(first, last):
                a_squares = two.tile([P, F], BF16, name="a_squares")
                nc.scalar.activation(
                    a_squares[:], a_ps[:, kb * F : (kb + 1) * F], FN.Square, accum_out=q[:, kb : kb + 1]
                )
            if on_scalar:
                nc.scalar.activation(root[:, blocks], q[:, blocks], FN.Sqrt)
            else:
                nc.gpsimd.tensor_tensor(root[:, blocks], q[:, blocks], plus_half[:, blocks], ALU.pow)
            nc.vector.tensor_scalar_add(inverse_of[:, blocks], q[:, blocks], 1.0)
            nc.vector.reciprocal(inverse_of[:, blocks], inverse_of[:, blocks])

        a0_ps = psum_a.tile([P, K], F32, name="a0_ps", tag="a")
        with tc.psum_pool(name="psum_h", bufs=3) as psum_h, tc.psum_pool(name="psum_u", bufs=4) as psum_u:
            b_all = held.tile([P, K], F32, name="b_all")
            with tc.tile_pool(name="adj", bufs=NCH) as adj_pool:
                adj_runs = adj_t.rearrange("(t p) j -> p t j", p=P)
                adj_chunks = []
                for c in range(NCH):
                    adj_c = adj_pool.tile([P, NB, CH], BF16, name="adj_c")
                    parts = [(0, HALF), (HALF, CH)] if c == 0 else [(0, CH)]
                    for lo, hi in parts:
                        for q in range(0, NB, BPC):
                            nc.sync.dma_start(adj_c[:, q : q + BPC, lo:hi], adj_runs[:, q : q + BPC, c * CH + lo : c * CH + hi])
                        if c == 0 and lo == 0:
                            nc.sync.dma_start(b_all[:], b.rearrange("k one -> (k one)").partition_broadcast(P))
                    adj_chunks.append(adj_c)
                nc.sync.dma_start(offsets[:], offs)

                h_pss, h_bfs, u_pss, us, exps = {}, {}, {}, {}, {}

                def aggregate(hc):
                    adj_half = adj_chunks[hc // 2][:, :, (hc % 2) * HALF : (hc % 2 + 1) * HALF]
                    h_pss[hc] = psum_h.tile([F, HALF], F32, name="h_ps", tag="h")
                    for t in range(NB):
                        nc.tensor.matmul(
                            h_pss[hc][:], lhsT=x_sb[:, t, :], rhs=adj_half[:, t, :], start=(t == 0), stop=(t == NB - 1)
                        )

                def round_h(hc):
                    h_bfs[hc] = four.tile([F, HALF], BF16, name="h_bf")
                    nc.scalar.copy(h_bfs[hc][:], h_pss[hc][:])

                def linear(hc):
                    for r, nb in enumerate(pairs[hc]):
                        u_pss[nb] = psum_u.tile([P, K], F32, name="u_ps", tag="u")
                        nc.tensor.matmul(
                            u_pss[nb][:], lhsT=h_bfs[hc][:, r * P : (r + 1) * P], rhs=w_sb[:], start=True, stop=True
                        )

                def add_bias(hc):
                    for nb in pairs[hc]:
                        us[nb] = four.tile([P, K], F32, name="u")
                        nc.vector.tensor_tensor(us[nb][:], u_pss[nb][:], b_all[:], ALU.add)

                def sums_of_squares(hc):
                    for nb in pairs[hc]:
                        squares = four.tile([P, K], BF16, name="squares")
                        nc.scalar.activation(
                            squares[:], us[nb][:], FN.Square, scale=math.sqrt(BN_EPS), accum_out=ssq[:, nb : nb + 1]
                        )

                def relu(hc):
                    for nb in pairs[hc]:
                        nc.vector.tensor_scalar_max(logits[nb][:], us[nb][:], 0.0)

                def statistics(hc):
                    for nb in pairs[hc]:
                        nc.vector.bn_stats(stats[:, nb, :], logits[nb][:])

                def mean_and_variance(hc):
                    for nb in pairs[hc]:
                        nc.vector.bn_aggr(mean_var[:, nb, :], stats[:, nb, :])

                def gains(hc):
                    blocks = columns(pairs[hc])
                    nc.vector.scalar_tensor_tensor(
                        spread[:, blocks], ssq[:, blocks], BN_EPS * NORM_EPS * NORM_EPS, mean_var[:, blocks, 1],
                        ALU.max, ALU.add,
                    )
                    nc.gpsimd.tensor_tensor(gain[:, blocks], spread[:, blocks], minus_half[:], ALU.pow)

                def shifts(hc):
                    blocks = columns(pairs[hc])
                    nc.vector.scalar_tensor_tensor(
                        shift[:, blocks], mean_var[:, blocks, 0], -1.0, gain[:, blocks], ALU.mult, ALU.mult
                    )

                def exponentials(hc):
                    for nb in pairs[hc]:
                        exps[nb] = four.tile([P, K], F32, name="e")
                        nc.scalar.activation(
                            exps[nb][:], logits[nb][:], FN.Exp, bias=shift[:, nb : nb + 1], scale=gain[:, nb : nb + 1],
                            accum_out=total[:, nb : nb + 1],
                        )

                def inverse_sums(hc):
                    nc.vector.reciprocal(inverse[:, columns(pairs[hc])], total[:, columns(pairs[hc])])

                def divide(hc):
                    divide_and_sum(pairs[hc], exps, a0_ps)

                for turn in range(-2, NH + 2):
                    run(linear, turn + 1)
                    run(aggregate, turn + 2)
                    run(add_bias, turn)
                    run(gains, turn - 1)
                    run(sums_of_squares, turn)
                    run(inverse_sums, turn - 2)
                    run(relu, turn)
                    run(divide, turn - 2)
                    run(statistics, turn)
                    run(shifts, turn - 1)
                    run(exponentials, turn - 1)
                    run(round_h, turn + 2)
                    run(mean_and_variance, turn)

        unread = held.tile([P, 2], F32, name="unread")
        nc.scalar.activation(unread[:, 0:1], total[:, NB - 1 : NB], FN.Sqrt)

        psum_r = ctx.enter_context(tc.psum_pool(name="psum_r", bufs=7))

        def capsules(a_ps, root, inverse_of, kb, cap_t, on_vector):
            cap = two.tile([P, F], BF16, name="cap")
            cap_ps = psum_r.tile([F, P], BF16, name="cap_ps", tag="r")
            if on_vector:
                nc.vector.tensor_scalar(
                    cap[:], a_ps[:, kb * F : (kb + 1) * F], root[:, kb : kb + 1], inverse_of[:, kb : kb + 1],
                    ALU.mult, ALU.mult,
                )
                nc.tensor.transpose(cap_ps[:], cap[:], ident_b[:])
                nc.vector.tensor_copy(cap_t, cap_ps[:])
            else:
                scaled = two.tile([P, F], F32, name="scaled")
                nc.scalar.activation(scaled[:], a_ps[:, kb * F : (kb + 1) * F], FN.Copy, scale=root[:, kb : kb + 1])
                nc.scalar.activation(cap[:], scaled[:], FN.Copy, scale=inverse_of[:, kb : kb + 1])
                nc.tensor.transpose(cap_ps[:], cap[:], ident_b[:])
                nc.scalar.copy(cap_t, cap_ps[:])

        for c in range(NCH):
            x_ps = psum_r.tile([F, CH], BF16, name="x_ps", tag="r")
            for r in range(BPC):
                nc.tensor.transpose(x_ps[:, r * P : (r + 1) * P], x_sb[:, c * BPC + r, :], ident_b[:])
            nc.vector.tensor_copy(x_t[:, c * CH : (c + 1) * CH], x_ps[:])

        late = ctx.enter_context(tc.tile_pool(name="late", bufs=1))
        windows = [late.tile([P, S], F32, name=f"window{kb}") for kb in range(KB)]
        for kb in range(KB):
            nc.sync.dma_start(windows[kb][:], base[kb * P : (kb + 1) * P, :])
        s1_t = [late.tile([P, N], F32, name=f"s1_t{kb}") for kb in range(KB)]

        early_ps = {}
        for nb in range(EARLY):
            nc.vector.tensor_scalar(
                logits[nb][:], logits[nb][:], gain[:, nb : nb + 1], shift[:, nb : nb + 1], ALU.mult, ALU.add
            )
            early_ps[nb] = psum_r.tile([P, K], F32, name="step_ps", tag="r")
            nc.tensor.matmul(early_ps[nb][:], lhsT=ident_f[:], rhs=logits[nb][:], start=True, stop=False)

        q0 = held.tile([P, KB], F32, name="q0")
        root0 = held.tile([P, KB], F32, name="root0")
        inverse_of0 = held.tile([P, KB], F32, name="inverse_of0")
        squash_factor(a0_ps, q0, root0, inverse_of0, 0, KB, on_scalar=True)
        nc.scalar.activation(unread[:, 1:2], root0[:, 0:1], FN.Exp, scale=0.0)
        cap0_t = held.tile([F, K], BF16, name="cap0_t")
        cap0_ps = psum_r.tile([F, K], BF16, name="cap0_ps", tag="r")
        for kb in range(KB):
            cap0 = four.tile([P, F], BF16, name="cap0")
            nc.vector.tensor_scalar(
                cap0[:], a0_ps[:, kb * F : (kb + 1) * F], root0[:, kb : kb + 1], inverse_of0[:, kb : kb + 1],
                ALU.mult, ALU.mult,
            )
            nc.tensor.transpose(cap0_ps[:, kb * P : (kb + 1) * P], cap0[:], ident_b[:])
        nc.vector.tensor_copy(cap0_t[:], cap0_ps[:])
        minus_gain = held.tile([P, NB], F32, name="minus_gain")
        nc.vector.tensor_scalar_mul(minus_gain[:], gain[:], -1.0)

        def transpose_s1(kb, c):
            turned = psum_r.tile([P, CH], F32, name="turned", tag="r")
            for r in range(BPC):
                nc.tensor.transpose(
                    turned[:, r * P : (r + 1) * P], logits[c * BPC + r][:, kb * P : (kb + 1) * P], ident_f[:]
                )
            nc.scalar.mul(s1_t[kb][:, c * CH : (c + 1) * CH], turned[:], -1.0)

        a1_ps = psum_a.tile([P, K], F32, name="a1_ps", tag="a")
        for c in range(NCH):
            for nb in range(c * BPC, (c + 1) * BPC):
                if nb < EARLY:
                    nc.tensor.matmul(
                        early_ps[nb][:], lhsT=x_t[:, nb * P : (nb + 1) * P], rhs=cap0_t[:], start=False, stop=True
                    )
                    nc.vector.tensor_scalar(
                        logits[nb][:], early_ps[nb][:], -1.0, None, ALU.mult, ALU.min, accum_out=minus_top[:, nb : nb + 1]
                    )
                else:
                    step_ps = psum_r.tile([P, K], F32, name="step_ps", tag="r")
                    nc.tensor.matmul(
                        step_ps[:], lhsT=x_t[:, nb * P : (nb + 1) * P], rhs=cap0_t[:], start=True, stop=True
                    )
                    partial = four.tile([P, K], F32, name="partial")
                    nc.vector.scalar_tensor_tensor(
                        partial[:], logits[nb][:], minus_gain[:, nb : nb + 1], step_ps[:], ALU.mult, ALU.subtract
                    )
                    nc.vector.tensor_scalar(
                        logits[nb][:], partial[:], shift[:, nb : nb + 1], None, ALU.subtract, ALU.min,
                        accum_out=minus_top[:, nb : nb + 1],
                    )
                exps[nb] = four.tile([P, K], F32, name="e")
                nc.scalar.activation(
                    exps[nb][:], logits[nb][:], FN.Exp, bias=minus_top[:, nb : nb + 1], scale=-1.0,
                    accum_out=total[:, nb : nb + 1],
                )
                nc.vector.reciprocal(inverse[:, nb : nb + 1], total[:, nb : nb + 1])
                divide_and_sum((nb,), exps, a1_ps)
        for c in range(NCH):
            transpose_s1(0, c)

        q1 = held.tile([P, KB], F32, name="q1")
        root1 = held.tile([P, KB], F32, name="root1")
        inverse_of1 = held.tile([P, KB], F32, name="inverse_of1")
        squash_factor(a1_ps, q1, root1, inverse_of1, 0, 1, on_scalar=False)
        squash_factor(a1_ps, q1, root1, inverse_of1, 1, KB, on_scalar=False)
        for kb in range(KB):
            cap1_t = two.tile([F, P], BF16, name="cap1_t")
            capsules(a1_ps, root1, inverse_of1, kb, cap1_t[:], on_vector=(kb == 0))
            if kb > 0:
                for c in range(NCH):
                    transpose_s1(kb, c)
            last_step = late.tile([P, N], F32, name="last_step", bufs=2)
            for c in range(NCH):
                last_ps = psum_r.tile([P, CH], F32, name="last_ps", tag="r")
                nc.tensor.matmul(
                    last_ps[:], lhsT=cap1_t[:], rhs=x_t[:, c * CH : (c + 1) * CH],
                    start=True, stop=True,
                )
                if kb == 0 and c % 2 == 1:
                    nc.vector.tensor_copy(last_step[:, c * CH : (c + 1) * CH], last_ps[:])
                else:
                    nc.scalar.copy(last_step[:, c * CH : (c + 1) * CH], last_ps[:])
            nc.vector.tensor_tensor(windows[kb][:].indirect(offsets[:]), s1_t[kb][:], last_step[:], ALU.add)
            nc.sync.dma_start(out[kb * P : (kb + 1) * P, :], windows[kb][:])
